import numpy as np
import ml_dtypes


def mxq(x, axis, fmt="e4m3"):
    dtype, down = {"e4m3": (ml_dtypes.float8_e4m3fn, 7), "e5m2": (ml_dtypes.float8_e5m2, 14)}[fmt]
    v = np.moveaxis(np.asarray(x, np.float32).astype(ml_dtypes.bfloat16).astype(np.float64), axis, -1)
    blocks = v.reshape(v.shape[:-1] + (-1, 32))
    amax = np.abs(blocks).max(-1, keepdims=True)
    byte = np.maximum(np.where(amax > 0, np.frexp(amax)[1] - 1 + 127, 0) - down, 1)
    scale = np.exp2(byte - 127.0)
    codes = (blocks / scale).astype(np.float32).astype(dtype).astype(np.float64)
    return np.moveaxis((codes * scale).reshape(v.shape), -1, axis)


WIDE = False


def mx_kscale(k):
    if not WIDE:
        return np.ones(k)
    levels = np.array([10, -10, 5, -5, 0])
    a = np.random.permutation(np.resize(levels, k // 512 * 4)).reshape(k // 512, 4)
    idx = np.arange(k)
    return np.exp2(a[idx // 512, idx % 128 // 32])


BF16 = ml_dtypes.bfloat16


def bf(x):
    return np.asarray(x, np.float32).astype(BF16)


def f64(x):
    return np.asarray(x).astype(np.float64)


B, N, C, O = 16, 512, 512, 512


def setup_inputs():
    t = mx_kscale(C)
    strength = (0.6 + 1.2 * np.random.random((B, N, 1))) * (np.random.random((B, N, 1)) >= 0.1)
    adj = np.random.random((B, N, N)) * strength * 100.0 / N
    feat = np.random.random((B, N, C)) * 2.0 * t
    return {"X": bf(np.concatenate([adj, feat], axis=2)), "W": bf(np.random.standard_normal((C, O)) * 1.5 / np.sqrt(C) / t[:, None])}


def reference(X, W):
    X = f64(X)
    A = X[:, :, :N]
    feat = X[:, :, N:]
    deg = A.sum(axis=2)
    d_inv_sqrt = np.where(deg > 0, 1.0 / np.sqrt(np.where(deg > 0, deg, 1.0)), 0.0)
    A_hat = A + np.eye(N)
    A_norm = d_inv_sqrt[:, :, None] * A_hat * d_inv_sqrt[:, None, :]
    h = mxq(A_norm, 2, "e4m3") @ mxq(feat, 1, "e4m3")
    return np.maximum(mxq(h, 2, "e4m3") @ mxq(f64(W), 0, "e4m3"), 0.0)

@@ -1,0 +1,235 @@
+import concourse.mybir as mybir
+from concourse.masks import make_identity
+
+FLOPS = 2 * 2 * 16 * 512 * 512 * 512
+
+BF16 = mybir.dt.bfloat16
+F32 = mybir.dt.float32
+U32 = mybir.dt.uint32
+U8 = mybir.dt.uint8
+FP8X4 = mybir.dt.float8_e4m3fn_x4
+ALU = mybir.AluOpType
+ACT = mybir.ActivationFunctionType
+
+P = 128
+PACK = 4
+GRAPHS = 16
+NODES = 512
+FEATS = 512
+OUTS = 512
+PAIR = 2
+HALVES = 2 * GRAPHS
+AHEAD = 3
+
+
+def tile_gcnconv_pa_t_kernel(tc, X, W, out):
+    nc = tc.nc
+    with tc.tile_pool(name="const", bufs=1) as const, tc.tile_pool(name="xin", bufs=AHEAD + 3) as xin, tc.tile_pool(
+        name="work", bufs=3
+    ) as work, tc.tile_pool(name="deep", bufs=6) as deep, tc.psum_pool(name="ps_d", bufs=1) as ps_d, tc.psum_pool(
+        name="ps_t", bufs=2
+    ) as ps_t, tc.psum_pool(name="ps_h", bufs=3) as ps_h, tc.psum_pool(name="ps_o", bufs=2) as ps_o, tc.manual_schedule():
+        kept = {}
+
+        def load(g):
+            x_sb = xin.tile([P, PACK, NODES + FEATS], BF16, name="x_sb")
+            nc.sync.dma_start(out=x_sb[:], in_=X[g].rearrange("(p j) w -> p j w", j=PACK))
+            kept[("x", g)] = x_sb
+
+        w_rows = const.tile([P, PACK, OUTS], BF16)
+        load(0)
+        nc.sync.dma_start(out=w_rows[:], in_=W.rearrange("(t p) o -> p t o", p=P))
+        for g in range(1, AHEAD):
+            load(g)
+
+        ident_f32 = const.tile([P, P], F32)
+        make_identity(nc, ident_f32[:])
+        ident_bf = const.tile([P, P], BF16)
+        make_identity(nc, ident_bf[:])
+
+        w_codes = const.tile([P, OUTS], U32, align_bytes=64)
+        w_scales = const.tile([P, OUTS], U8, align_bytes=64)
+
+        def prepare_w():
+            w_grouped = const.tile([P, OUTS, PACK], BF16, align_bytes=64)
+            nc.vector.tensor_copy(out=w_grouped[:], in_=w_rows[:].rearrange("p t o -> p o t"))
+            nc.vector.quantize_mx(
+                out=w_codes[:].bitcast(FP8X4), scales=w_scales[:], in_=w_grouped[:].rearrange("p o t -> p (o t)")
+            )
+
+        def quantise(pool, grouped, name):
+            codes = pool.tile([P, PAIR * P], U32, align_bytes=64, name=name + "_codes")
+            scales = pool.tile([P, PAIR * P], U8, align_bytes=64, name=name + "_scales")
+            nc.vector.quantize_mx(out=codes[:].bitcast(FP8X4), scales=scales[:], in_=grouped)
+            return codes, scales
+
+        def a_columns(g, j):
+            return kept[("x", g)][:, j, 0:NODES].rearrange("p (q t) -> p t q", t=PACK)
+
+        def degrees(g, half):
+            if half == 0:
+                kept[("deg", g)] = work.tile([P, PACK], F32, name="deg")
+                kept[("a_plus_i", g)] = deep.tile([P, PACK, P], F32, name="a_plus_i")
+            for j in range(half * PAIR, (half + 1) * PAIR):
+                unused = work.tile([P, NODES], BF16, name="unused")
+                nc.vector.tensor_scalar(
+                    out=unused[:],
+                    in0=kept[("x", g)][:, j, 0:NODES],
+                    scalar1=1.0,
+                    scalar2=None,
+                    op0=ALU.mult,
+                    op1=ALU.add,
+                    accum_out=kept[("deg", g)][:, j : j + 1],
+                )
+                nc.gpsimd.tensor_tensor(
+                    out=kept[("a_plus_i", g)][:, j, :], in0=a_columns(g, j)[:, j, :], in1=ident_f32[:], op=ALU.add
+                )
+
+        def roots(g):
+            deg = kept[("deg", g)]
+            safe = work.tile([P, PACK], F32, name="safe")
+            nc.vector.scalar_tensor_tensor(
+                out=safe[:], in0=deg[:], scalar=0.0, in1=deg[:], op0=ALU.is_le, op1=ALU.max
+            )
+            root = work.tile([P, PACK], F32, name="root")
+            nc.scalar.sqrt(root[:], safe[:])
+            kept[("root", g)] = root
+
+        def inverse_roots(g):
+            inv = work.tile([P, PACK], F32, name="inv")
+            nc.vector.reciprocal(inv[:], kept[("root", g)][:])
+            d = work.tile([P, PACK], F32, name="d")
+            nc.vector.scalar_tensor_tensor(
+                out=d[:], in0=kept[("deg", g)][:], scalar=0.0, in1=inv[:], op0=ALU.is_gt, op1=ALU.mult
+            )
+            d_free = ps_d.tile([P, PACK, P], F32, name="d_free")
+            for t in range(PACK):
+                nc.tensor.matmul(
+                    out=d_free[:, t, :],
+                    lhsT=d[:, t : t + 1].to_broadcast([P, P]),
+                    rhs=ident_f32[:],
+                    start=True,
+                    stop=True,
+                )
+            kept[("d", g)] = d
+            kept[("d_free", g)] = d_free
+
+        def regroup_feat(g, half):
+            f_grouped = work.tile([P, FEATS // 2, PACK], BF16, align_bytes=64, name="f_grouped")
+            first = NODES + half * (FEATS // 2)
+            nc.vector.tensor_copy(
+                out=f_grouped[:].rearrange("p (c i) j -> p c j i", i=4),
+                in_=kept[("x", g)][:, :, first : first + FEATS // 2].rearrange("p j (c i) -> p c j i", i=4),
+            )
+            kept[("f_grouped", g, half)] = f_grouped
+
+        def quantise_feat(g, half):
+            kept[("f", g, half)] = quantise(deep, kept[("f_grouped", g, half)][:].rearrange("p c j -> p (c j)"), "f")
+
+        def normalise(g, half):
+            d = kept[("d", g)]
+            d_free = kept[("d_free", g)]
+            a_norm = work.tile([P, PAIR, PACK, P], BF16, name="a_norm")
+            for a in range(PAIR):
+                j = half * PAIR + a
+                nc.vector.scalar_tensor_tensor(
+                    out=a_norm[:, a, j, :],
+                    in0=kept[("a_plus_i", g)][:, j, :],
+                    scalar=d[:, j : j + 1],
+                    in1=d_free[:, j, :],
+                    op0=ALU.mult,
+                    op1=ALU.mult,
+                )
+                for t0, t1 in ((0, j), (j + 1, PACK)):
+                    if t1 > t0:
+                        nc.vector.scalar_tensor_tensor(
+                            out=a_norm[:, a, t0:t1, :],
+                            in0=a_columns(g, j)[:, t0:t1, :],
+                            scalar=d[:, j : j + 1],
+                            in1=d_free[:, t0:t1, :],
+                            op0=ALU.mult,
+                            op1=ALU.mult,
+                        )
+            kept[("a_norm", g, half)] = a_norm
+
+        def transpose(g, half):
+            a_norm = kept[("a_norm", g, half)]
+            a_t = ps_t.tile([P, PAIR, PACK, P], BF16, name="a_t")
+            for a in range(PAIR):
+                for t in range(PACK):
+                    nc.tensor.transpose(a_t[:, a, t, :], a_norm[:, a, t, :], ident_bf[:])
+            a_grouped = work.tile([P, PAIR, P, PACK], BF16, align_bytes=64, name="a_grouped")
+            nc.scalar.copy(out=a_grouped[:], in_=a_t[:].rearrange("p a t n -> p a n t"))
+            kept[("a_grouped", g, half)] = a_grouped
+
+        def quantise_a(g, half):
+            kept[("a", g, half)] = quantise(work, kept[("a_grouped", g, half)][:].rearrange("p a n t -> p (a n t)"), "a")
+            kept[("h_grouped", g, half)] = work.tile([P, PAIR, P, PACK], BF16, align_bytes=64, name="h_grouped")
+
+        def first_product(g, half, a):
+            a_codes, a_scales = kept[("a", g, half)]
+            h_t = ps_h.tile([P, PACK, P], F32, name="h_t")
+            for t in range(PACK):
+                f_codes, f_scales = kept[("f", g, t // PAIR)]
+                f_cols = slice((t % PAIR) * P, (t % PAIR + 1) * P)
+                nc.tensor.matmul_mx(
+                    out=h_t[:, t, :],
+                    lhsT=f_codes[:, f_cols].bitcast(FP8X4),
+                    lhsT_scale=f_scales[:, f_cols],
+                    rhs=a_codes[:, a * P : (a + 1) * P].bitcast(FP8X4),
+                    rhs_scale=a_scales[:, a * P : (a + 1) * P],
+                    start=True,
+                    stop=True,
+                )
+            nc.scalar.copy(out=kept[("h_grouped", g, half)][:, a, :, :], in_=h_t[:].rearrange("p t n -> p n t"))
+
+        def quantise_h(g, half):
+            kept[("h", g, half)] = quantise(work, kept[("h_grouped", g, half)][:].rearrange("p a n t -> p (a n t)"), "h")
+            kept[("result", g, half)] = work.tile([P, PAIR, OUTS], F32, name="result")
+
+        def second_product(g, half, a):
+            h_codes, h_scales = kept[("h", g, half)]
+            o_ps = ps_o.tile([P, OUTS], F32, name="o_ps")
+            nc.tensor.matmul_mx(
+                out=o_ps[:],
+                lhsT=h_codes[:, a * P : (a + 1) * P].bitcast(FP8X4),
+                lhsT_scale=h_scales[:, a * P : (a + 1) * P],
+                rhs=w_codes[:].bitcast(FP8X4),
+                rhs_scale=w_scales[:],
+                start=True,
+                stop=True,
+            )
+            nc.scalar.activation(out=kept[("result", g, half)][:, a, :], in_=o_ps[:], func=ACT.Relu)
+
+        def store(g, half):
+            out_rows = out[g].rearrange("(p j) o -> p j o", j=PACK)
+            nc.sync.dma_start(out=out_rows[:, half * PAIR : (half + 1) * PAIR, :], in_=kept[("result", g, half)][:])
+
+        def at(u, stage):
+            if 0 <= u < HALVES:
+                stage(u // 2, u % 2)
+
+        def tick(s):
+            if s % 2 == 0 and s // 2 + AHEAD < GRAPHS:
+                load(s // 2 + AHEAD)
+            at(s - 3, normalise)
+            for a in range(PAIR):
+                at(s - 8, lambda g, half: second_product(g, half, a))
+                at(s - 6, lambda g, half: first_product(g, half, a))
+                if a == 0:
+                    at(s - 4, transpose)
+            at(s - 8, store)
+            at(s, degrees)
+            if s % 2 == 1 and s // 2 < GRAPHS:
+                roots(s // 2)
+            if s % 2 == 0 and 0 <= s // 2 - 1 < GRAPHS:
+                inverse_roots(s // 2 - 1)
+            at(s - 5, quantise_a)
+            at(s - 7, quantise_h)
+            at(s - 3, regroup_feat)
+            at(s - 4, quantise_feat)
+
+        for s in range(HALVES + 8):
+            tick(s)
+            if s == 2:
+                prepare_w()

@@ -81,7 +81,7 @@ def tile_gcnconv_pa_t_kernel(tc, X, W, out):
                     op1=ALU.add,
                     accum_out=kept[("deg", g)][:, j : j + 1],
                 )
-                nc.gpsimd.tensor_tensor(
+                nc.vector.tensor_tensor(
                     out=kept[("a_plus_i", g)][:, j, :], in0=a_columns(g, j)[:, j, :], in1=ident_f32[:], op=ALU.add
                 )
 

@@ -81,7 +81,7 @@ def tile_gcnconv_pa_t_kernel(tc, X, W, out):
                     op1=ALU.add,
                     accum_out=kept[("deg", g)][:, j : j + 1],
                 )
-                nc.vector.tensor_tensor(
+                nc.gpsimd.tensor_tensor(
                     out=kept[("a_plus_i", g)][:, j, :], in0=a_columns(g, j)[:, j, :], in1=ident_f32[:], op=ALU.add
                 )
 
@@ -104,13 +104,7 @@ def tile_gcnconv_pa_t_kernel(tc, X, W, out):
             )
             d_free = ps_d.tile([P, PACK, P], F32, name="d_free")
             for t in range(PACK):
-                nc.tensor.matmul(
-                    out=d_free[:, t, :],
-                    lhsT=d[:, t : t + 1].to_broadcast([P, P]),
-                    rhs=ident_f32[:],
-                    start=True,
-                    stop=True,
-                )
+                nc.tensor.transpose(d_free[:, t, :], d[:, t : t + 1].to_broadcast([P, P]), ident_f32[:])
             kept[("d", g)] = d
             kept[("d_free", g)] = d_free
 
@@ -216,9 +210,8 @@ def tile_gcnconv_pa_t_kernel(tc, X, W, out):
             for a in range(PAIR):
                 at(s - 8, lambda g, half: second_product(g, half, a))
                 at(s - 6, lambda g, half: first_product(g, half, a))
-                if a == 0:
-                    at(s - 4, transpose)
             at(s - 8, store)
+            at(s - 4, transpose)
             at(s, degrees)
             if s % 2 == 1 and s // 2 < GRAPHS:
                 roots(s // 2)

@@ -31,16 +31,17 @@ def tile_gcnconv_pa_t_kernel(tc, X, W, out):
     ) as ps_t, tc.psum_pool(name="ps_h", bufs=3) as ps_h, tc.psum_pool(name="ps_o", bufs=2) as ps_o, tc.manual_schedule():
         kept = {}
 
-        def load(g):
-            x_sb = xin.tile([P, PACK, NODES + FEATS], BF16, name="x_sb")
-            nc.sync.dma_start(out=x_sb[:], in_=X[g].rearrange("(p j) w -> p j w", j=PACK))
-            kept[("x", g)] = x_sb
+        def load(g, half):
+            if half == 0:
+                kept[("x", g)] = xin.tile([P, PACK, NODES + FEATS], BF16, name="x_sb")
+            rows = slice(half * PAIR, (half + 1) * PAIR)
+            nc.sync.dma_start(out=kept[("x", g)][:, rows, :], in_=X[g].rearrange("(p j) w -> p j w", j=PACK)[:, rows, :])
 
         w_rows = const.tile([P, PACK, OUTS], BF16)
-        load(0)
-        nc.sync.dma_start(out=w_rows[:], in_=W.rearrange("(t p) o -> p t o", p=P))
-        for g in range(1, AHEAD):
-            load(g)
+        for u in range(2 * AHEAD):
+            load(u // 2, u % 2)
+            if u == 1:
+                nc.sync.dma_start(out=w_rows[:], in_=W.rearrange("(t p) o -> p t o", p=P))
 
         ident_f32 = const.tile([P, P], F32)
         make_identity(nc, ident_f32[:])
@@ -52,7 +53,14 @@ def tile_gcnconv_pa_t_kernel(tc, X, W, out):
 
         def prepare_w():
             w_grouped = const.tile([P, OUTS, PACK], BF16, align_bytes=64)
-            nc.vector.tensor_copy(out=w_grouped[:], in_=w_rows[:].rearrange("p t o -> p o t"))
+            nc.gpsimd.tensor_scalar(
+                out=w_grouped[:],
+                in0=w_rows[:].rearrange("p t o -> p o t"),
+                scalar1=1.0,
+                scalar2=0.0,
+                op0=ALU.mult,
+                op1=ALU.add,
+            )
             nc.vector.quantize_mx(
                 out=w_codes[:].bitcast(FP8X4), scales=w_scales[:], in_=w_grouped[:].rearrange("p o t -> p (o t)")
             )
@@ -102,10 +110,13 @@ def tile_gcnconv_pa_t_kernel(tc, X, W, out):
             nc.vector.scalar_tensor_tensor(
                 out=d[:], in0=kept[("deg", g)][:], scalar=0.0, in1=inv[:], op0=ALU.is_gt, op1=ALU.mult
             )
+            kept[("d", g)] = d
+
+        def spread(g):
+            d = kept[("d", g)]
             d_free = ps_d.tile([P, PACK, P], F32, name="d_free")
             for t in range(PACK):
                 nc.tensor.transpose(d_free[:, t, :], d[:, t : t + 1].to_broadcast([P, P]), ident_f32[:])
-            kept[("d", g)] = d
             kept[("d_free", g)] = d_free
 
         def regroup_feat(g, half):
@@ -204,25 +215,27 @@ def tile_gcnconv_pa_t_kernel(tc, X, W, out):
                 stage(u // 2, u % 2)
 
         def tick(s):
-            if s % 2 == 0 and s // 2 + AHEAD < GRAPHS:
-                load(s // 2 + AHEAD)
+            at(s + 2 * AHEAD, load)
             at(s - 3, normalise)
+            ready = s % 2 == 0 and 0 <= s // 2 - 1 < GRAPHS
+            if ready:
+                inverse_roots(s // 2 - 1)
             for a in range(PAIR):
-                at(s - 8, lambda g, half: second_product(g, half, a))
-                at(s - 6, lambda g, half: first_product(g, half, a))
-            at(s - 8, store)
-            at(s - 4, transpose)
+                at(s - 6, lambda g, half: second_product(g, half, a))
+                at(s - 5, lambda g, half: first_product(g, half, a))
+            at(s - 6, store)
+            if ready:
+                spread(s // 2 - 1)
+            at(s - 3, transpose)
             at(s, degrees)
             if s % 2 == 1 and s // 2 < GRAPHS:
                 roots(s // 2)
-            if s % 2 == 0 and 0 <= s // 2 - 1 < GRAPHS:
-                inverse_roots(s // 2 - 1)
-            at(s - 5, quantise_a)
-            at(s - 7, quantise_h)
-            at(s - 3, regroup_feat)
-            at(s - 4, quantise_feat)
+            at(s - 4, quantise_a)
+            at(s - 2, regroup_feat)
+            at(s - 3, quantise_feat)
+            at(s - 5, quantise_h)
 
-        for s in range(HALVES + 8):
+        for s in range(HALVES + 6):
             tick(s)
             if s == 2:
                 prepare_w()

@@ -51,8 +51,9 @@ def tile_gcnconv_pa_t_kernel(tc, X, W, out):
         w_codes = const.tile([P, OUTS], U32, align_bytes=64)
         w_scales = const.tile([P, OUTS], U8, align_bytes=64)
 
-        def prepare_w():
-            w_grouped = const.tile([P, OUTS, PACK], BF16, align_bytes=64)
+        w_grouped = const.tile([P, OUTS, PACK], BF16, align_bytes=64)
+
+        def regroup_w():
             nc.gpsimd.tensor_scalar(
                 out=w_grouped[:],
                 in0=w_rows[:].rearrange("p t o -> p o t"),
@@ -61,6 +62,8 @@ def tile_gcnconv_pa_t_kernel(tc, X, W, out):
                 op0=ALU.mult,
                 op1=ALU.add,
             )
+
+        def quantise_w():
             nc.vector.quantize_mx(
                 out=w_codes[:].bitcast(FP8X4), scales=w_scales[:], in_=w_grouped[:].rearrange("p o t -> p (o t)")
             )
@@ -171,7 +174,7 @@ def tile_gcnconv_pa_t_kernel(tc, X, W, out):
             kept[("a", g, half)] = quantise(work, kept[("a_grouped", g, half)][:].rearrange("p a n t -> p (a n t)"), "a")
             kept[("h_grouped", g, half)] = work.tile([P, PAIR, P, PACK], BF16, align_bytes=64, name="h_grouped")
 
-        def first_product(g, half, a):
+        def first_product(g, half, a, on_vector):
             a_codes, a_scales = kept[("a", g, half)]
             h_t = ps_h.tile([P, PACK, P], F32, name="h_t")
             for t in range(PACK):
@@ -186,13 +189,18 @@ def tile_gcnconv_pa_t_kernel(tc, X, W, out):
                     start=True,
                     stop=True,
                 )
-            nc.scalar.copy(out=kept[("h_grouped", g, half)][:, a, :, :], in_=h_t[:].rearrange("p t n -> p n t"))
+            if on_vector:
+                nc.vector.tensor_copy(
+                    out=kept[("h_grouped", g, half)][:, a, :, :], in_=h_t[:].rearrange("p t n -> p n t")
+                )
+            else:
+                nc.scalar.copy(out=kept[("h_grouped", g, half)][:, a, :, :], in_=h_t[:].rearrange("p t n -> p n t"))
 
         def quantise_h(g, half):
             kept[("h", g, half)] = quantise(work, kept[("h_grouped", g, half)][:].rearrange("p a n t -> p (a n t)"), "h")
             kept[("result", g, half)] = work.tile([P, PAIR, OUTS], F32, name="result")
 
-        def second_product(g, half, a):
+        def second_product(g, half, a, on_vector):
             h_codes, h_scales = kept[("h", g, half)]
             o_ps = ps_o.tile([P, OUTS], F32, name="o_ps")
             nc.tensor.matmul_mx(
@@ -204,7 +212,10 @@ def tile_gcnconv_pa_t_kernel(tc, X, W, out):
                 start=True,
                 stop=True,
             )
-            nc.scalar.activation(out=kept[("result", g, half)][:, a, :], in_=o_ps[:], func=ACT.Relu)
+            if on_vector:
+                nc.vector.tensor_scalar_max(out=kept[("result", g, half)][:, a, :], in0=o_ps[:], scalar1=0.0)
+            else:
+                nc.scalar.activation(out=kept[("result", g, half)][:, a, :], in_=o_ps[:], func=ACT.Relu)
 
         def store(g, half):
             out_rows = out[g].rearrange("(p j) o -> p j o", j=PACK)
@@ -215,27 +226,29 @@ def tile_gcnconv_pa_t_kernel(tc, X, W, out):
                 stage(u // 2, u % 2)
 
         def tick(s):
+            draining = s - 3 >= HALVES
             at(s + 2 * AHEAD, load)
-            at(s - 3, normalise)
-            ready = s % 2 == 0 and 0 <= s // 2 - 1 < GRAPHS
-            if ready:
-                inverse_roots(s // 2 - 1)
+            at(s - 5, quantise_a)
+            at(s - 6, quantise_h)
+            at(s - 4, transpose)
             for a in range(PAIR):
-                at(s - 6, lambda g, half: second_product(g, half, a))
-                at(s - 5, lambda g, half: first_product(g, half, a))
+                at(s - 5, lambda g, half: first_product(g, half, a, draining and a == 1))
+            for a in range(PAIR):
+                at(s - 6, lambda g, half: second_product(g, half, a, draining and a == 1))
             at(s - 6, store)
-            if ready:
+            at(s - 3, normalise)
+            if s % 2 == 0 and 0 <= s // 2 - 1 < GRAPHS:
+                inverse_roots(s // 2 - 1)
                 spread(s // 2 - 1)
-            at(s - 3, transpose)
             at(s, degrees)
             if s % 2 == 1 and s // 2 < GRAPHS:
                 roots(s // 2)
-            at(s - 4, quantise_a)
             at(s - 2, regroup_feat)
             at(s - 3, quantise_feat)
-            at(s - 5, quantise_h)
 
         for s in range(HALVES + 6):
             tick(s)
             if s == 2:
-                prepare_w()
+                regroup_w()
+            if s == 5:
+                quantise_w()

@@ -125,9 +125,13 @@ def tile_gcnconv_pa_t_kernel(tc, X, W, out):
         def regroup_feat(g, half):
             f_grouped = work.tile([P, FEATS // 2, PACK], BF16, align_bytes=64, name="f_grouped")
             first = NODES + half * (FEATS // 2)
-            nc.vector.tensor_copy(
-                out=f_grouped[:].rearrange("p (c i) j -> p c j i", i=4),
-                in_=kept[("x", g)][:, :, first : first + FEATS // 2].rearrange("p j (c i) -> p c j i", i=4),
+            nc.gpsimd.tensor_scalar(
+                out=f_grouped[:],
+                in0=kept[("x", g)][:, :, first : first + FEATS // 2].rearrange("p j c -> p c j"),
+                scalar1=1.0,
+                scalar2=0.0,
+                op0=ALU.mult,
+                op1=ALU.add,
             )
             kept[("f_grouped", g, half)] = f_grouped
 

@@ -33,9 +33,16 @@ def tile_gcnconv_pa_t_kernel(tc, X, W, out):
 
         def load(g, half):
             if half == 0:
-                kept[("x", g)] = xin.tile([P, PACK, NODES + FEATS], BF16, name="x_sb")
-            rows = slice(half * PAIR, (half + 1) * PAIR)
-            nc.sync.dma_start(out=kept[("x", g)][:, rows, :], in_=X[g].rearrange("(p j) w -> p j w", j=PACK)[:, rows, :])
+                kept[("a_sb", g)] = xin.tile([P, PACK, NODES], BF16, name="a_sb")
+                kept[("f_sb", g)] = xin.tile([P, PACK, FEATS], BF16, name="f_sb")
+            slots = slice(half * PAIR, (half + 1) * PAIR)
+            rows = slice(half * PAIR * P, (half + 1) * PAIR * P)
+            nc.sync.dma_start(
+                out=kept[("a_sb", g)][:, slots, :], in_=X[g, rows, 0:NODES].rearrange("(j p) m -> p j m", j=PAIR)
+            )
+            nc.sync.dma_start(
+                out=kept[("f_sb", g)][:, slots, :], in_=X[g, rows, NODES:].rearrange("(p e) c -> p e c", e=PAIR)
+            )
 
         w_rows = const.tile([P, PACK, OUTS], BF16)
         for u in range(2 * AHEAD):
@@ -45,8 +52,6 @@ def tile_gcnconv_pa_t_kernel(tc, X, W, out):
 
         ident_f32 = const.tile([P, P], F32)
         make_identity(nc, ident_f32[:])
-        ident_bf = const.tile([P, P], BF16)
-        make_identity(nc, ident_bf[:])
 
         w_codes = const.tile([P, OUTS], U32, align_bytes=64)
         w_scales = const.tile([P, OUTS], U8, align_bytes=64)
@@ -74,9 +79,6 @@ def tile_gcnconv_pa_t_kernel(tc, X, W, out):
             nc.vector.quantize_mx(out=codes[:].bitcast(FP8X4), scales=scales[:], in_=grouped)
             return codes, scales
 
-        def a_columns(g, j):
-            return kept[("x", g)][:, j, 0:NODES].rearrange("p (q t) -> p t q", t=PACK)
-
         def degrees(g, half):
             if half == 0:
                 kept[("deg", g)] = work.tile([P, PACK], F32, name="deg")
@@ -85,7 +87,7 @@ def tile_gcnconv_pa_t_kernel(tc, X, W, out):
                 unused = work.tile([P, NODES], BF16, name="unused")
                 nc.vector.tensor_scalar(
                     out=unused[:],
-                    in0=kept[("x", g)][:, j, 0:NODES],
+                    in0=kept[("a_sb", g)][:, j, :],
                     scalar1=1.0,
                     scalar2=None,
                     op0=ALU.mult,
@@ -93,7 +95,10 @@ def tile_gcnconv_pa_t_kernel(tc, X, W, out):
                     accum_out=kept[("deg", g)][:, j : j + 1],
                 )
                 nc.gpsimd.tensor_tensor(
-                    out=kept[("a_plus_i", g)][:, j, :], in0=a_columns(g, j)[:, j, :], in1=ident_f32[:], op=ALU.add
+                    out=kept[("a_plus_i", g)][:, j, :],
+                    in0=kept[("a_sb", g)][:, j, j * P : (j + 1) * P],
+                    in1=ident_f32[:],
+                    op=ALU.add,
                 )
 
         def roots(g):
@@ -117,17 +122,17 @@ def tile_gcnconv_pa_t_kernel(tc, X, W, out):
 
         def spread(g):
             d = kept[("d", g)]
-            d_free = ps_d.tile([P, PACK, P], F32, name="d_free")
-            for t in range(PACK):
-                nc.tensor.transpose(d_free[:, t, :], d[:, t : t + 1].to_broadcast([P, P]), ident_f32[:])
+            d_free = ps_d.tile([P, NODES], F32, name="d_free")
+            for j in range(PACK):
+                nc.tensor.transpose(d_free[:, j * P : (j + 1) * P], d[:, j : j + 1].to_broadcast([P, P]), ident_f32[:])
             kept[("d_free", g)] = d_free
 
         def regroup_feat(g, half):
             f_grouped = work.tile([P, FEATS // 2, PACK], BF16, align_bytes=64, name="f_grouped")
-            first = NODES + half * (FEATS // 2)
+            first = half * (FEATS // 2)
             nc.gpsimd.tensor_scalar(
                 out=f_grouped[:],
-                in0=kept[("x", g)][:, :, first : first + FEATS // 2].rearrange("p j c -> p c j"),
+                in0=kept[("f_sb", g)][:, :, first : first + FEATS // 2].rearrange("p t c -> p c t"),
                 scalar1=1.0,
                 scalar2=0.0,
                 op0=ALU.mult,
@@ -141,37 +146,41 @@ def tile_gcnconv_pa_t_kernel(tc, X, W, out):
         def normalise(g, half):
             d = kept[("d", g)]
             d_free = kept[("d_free", g)]
-            a_norm = work.tile([P, PAIR, PACK, P], BF16, name="a_norm")
+            a_norm = work.tile([P, PAIR, NODES], BF16, name="a_norm")
             for a in range(PAIR):
                 j = half * PAIR + a
-                nc.vector.scalar_tensor_tensor(
-                    out=a_norm[:, a, j, :],
-                    in0=kept[("a_plus_i", g)][:, j, :],
-                    scalar=d[:, j : j + 1],
-                    in1=d_free[:, j, :],
-                    op0=ALU.mult,
-                    op1=ALU.mult,
-                )
-                for t0, t1 in ((0, j), (j + 1, PACK)):
-                    if t1 > t0:
-                        nc.vector.scalar_tensor_tensor(
-                            out=a_norm[:, a, t0:t1, :],
-                            in0=a_columns(g, j)[:, t0:t1, :],
-                            scalar=d[:, j : j + 1],
-                            in1=d_free[:, t0:t1, :],
-                            op0=ALU.mult,
-                            op1=ALU.mult,
-                        )
+                diagonal = slice(j * P, (j + 1) * P)
+                pieces = [(diagonal, kept[("a_plus_i", g)][:, j, :])]
+                for cols in (slice(0, j * P), slice((j + 1) * P, NODES)):
+                    if cols.stop > cols.start:
+                        pieces.append((cols, kept[("a_sb", g)][:, j, cols]))
+                for cols, a_piece in pieces:
+                    nc.vector.scalar_tensor_tensor(
+                        out=a_norm[:, a, cols],
+                        in0=a_piece,
+                        scalar=d[:, j : j + 1],
+                        in1=d_free[:, cols],
+                        op0=ALU.mult,
+                        op1=ALU.mult,
+                    )
             kept[("a_norm", g, half)] = a_norm
 
         def transpose(g, half):
             a_norm = kept[("a_norm", g, half)]
-            a_t = ps_t.tile([P, PAIR, PACK, P], BF16, name="a_t")
+            words = a_norm[:].rearrange("p a m -> p (a m)").bitcast(F32)
+            a_t = ps_t.tile([P, PAIR, 2, P], F32, name="a_t")
             for a in range(PAIR):
-                for t in range(PACK):
-                    nc.tensor.transpose(a_t[:, a, t, :], a_norm[:, a, t, :], ident_bf[:])
+                for u in range(2):
+                    first = (2 * a + u) * P
+                    nc.tensor.transpose(a_t[:, a, u, :], words[:, first : first + P], ident_f32[:])
             a_grouped = work.tile([P, PAIR, P, PACK], BF16, align_bytes=64, name="a_grouped")
-            nc.scalar.copy(out=a_grouped[:], in_=a_t[:].rearrange("p a t n -> p a n t"))
+            nc.scalar.copy(
+                out=a_grouped[:]
+                .rearrange("p a n t -> p (a n t)")
+                .bitcast(F32)
+                .rearrange("p (a n u) -> p a n u", a=PAIR, u=2),
+                in_=a_t[:].rearrange("p a u n -> p a n u"),
+            )
             kept[("a_grouped", g, half)] = a_grouped
 
         def quantise_a(g, half):
@@ -222,7 +231,7 @@ def tile_gcnconv_pa_t_kernel(tc, X, W, out):
                 nc.scalar.activation(out=kept[("result", g, half)][:, a, :], in_=o_ps[:], func=ACT.Relu)
 
         def store(g, half):
-            out_rows = out[g].rearrange("(p j) o -> p j o", j=PACK)
+            out_rows = out[g].rearrange("(j p) o -> p j o", j=PACK)
             nc.sync.dma_start(out=out_rows[:, half * PAIR : (half + 1) * PAIR, :], in_=kept[("result", g, half)][:])
 
         def at(u, stage):

@@ -26,7 +26,7 @@ def tile_gcnconv_pa_t_kernel(tc, X, W, out):
     nc = tc.nc
     with tc.tile_pool(name="const", bufs=1) as const, tc.tile_pool(name="xin", bufs=AHEAD + 3) as xin, tc.tile_pool(
         name="work", bufs=3
-    ) as work, tc.tile_pool(name="deep", bufs=6) as deep, tc.psum_pool(name="ps_d", bufs=1) as ps_d, tc.psum_pool(
+    ) as work, tc.tile_pool(name="deep", bufs=6) as deep, tc.tile_pool(name="single", bufs=1) as single, tc.psum_pool(name="ps_d", bufs=1) as ps_d, tc.psum_pool(
         name="ps_t", bufs=2
     ) as ps_t, tc.psum_pool(name="ps_h", bufs=3) as ps_h, tc.psum_pool(name="ps_o", bufs=2) as ps_o, tc.manual_schedule():
         kept = {}
@@ -107,16 +107,22 @@ def tile_gcnconv_pa_t_kernel(tc, X, W, out):
             nc.vector.scalar_tensor_tensor(
                 out=safe[:], in0=deg[:], scalar=0.0, in1=deg[:], op0=ALU.is_le, op1=ALU.max
             )
+            kept[("safe", g)] = safe
+
+        def take_roots(g):
             root = work.tile([P, PACK], F32, name="root")
-            nc.scalar.sqrt(root[:], safe[:])
+            nc.scalar.sqrt(root[:], kept[("safe", g)][:])
             kept[("root", g)] = root
 
         def inverse_roots(g):
             inv = work.tile([P, PACK], F32, name="inv")
             nc.vector.reciprocal(inv[:], kept[("root", g)][:])
+            kept[("inv", g)] = inv
+
+        def mask_roots(g):
             d = work.tile([P, PACK], F32, name="d")
             nc.vector.scalar_tensor_tensor(
-                out=d[:], in0=kept[("deg", g)][:], scalar=0.0, in1=inv[:], op0=ALU.is_gt, op1=ALU.mult
+                out=d[:], in0=kept[("deg", g)][:], scalar=0.0, in1=kept[("inv", g)][:], op0=ALU.is_gt, op1=ALU.mult
             )
             kept[("d", g)] = d
 
@@ -128,7 +134,7 @@ def tile_gcnconv_pa_t_kernel(tc, X, W, out):
             kept[("d_free", g)] = d_free
 
         def regroup_feat(g, half):
-            f_grouped = work.tile([P, FEATS // 2, PACK], BF16, align_bytes=64, name="f_grouped")
+            f_grouped = single.tile([P, FEATS // 2, PACK], BF16, align_bytes=64, name="f_grouped")
             first = half * (FEATS // 2)
             nc.gpsimd.tensor_scalar(
                 out=f_grouped[:],
@@ -241,23 +247,31 @@ def tile_gcnconv_pa_t_kernel(tc, X, W, out):
         def tick(s):
             draining = s - 3 >= HALVES
             at(s + 2 * AHEAD, load)
+            g_d = s // 2 - 1
+            even = s % 2 == 0 and 0 <= g_d < GRAPHS
+            odd = s % 2 == 1 and 0 <= g_d < GRAPHS
+            if even:
+                roots(g_d)
+            if odd:
+                mask_roots(g_d)
             at(s - 5, quantise_a)
             at(s - 6, quantise_h)
+            at(s - 3, quantise_feat)
             at(s - 4, transpose)
+            if even:
+                take_roots(g_d)
+            if odd:
+                spread(g_d)
             for a in range(PAIR):
                 at(s - 5, lambda g, half: first_product(g, half, a, draining and a == 1))
             for a in range(PAIR):
                 at(s - 6, lambda g, half: second_product(g, half, a, draining and a == 1))
             at(s - 6, store)
             at(s - 3, normalise)
-            if s % 2 == 0 and 0 <= s // 2 - 1 < GRAPHS:
-                inverse_roots(s // 2 - 1)
-                spread(s // 2 - 1)
-            at(s, degrees)
-            if s % 2 == 1 and s // 2 < GRAPHS:
-                roots(s // 2)
+            if even:
+                inverse_roots(g_d)
             at(s - 2, regroup_feat)
-            at(s - 3, quantise_feat)
+            at(s, degrees)
 
         for s in range(HALVES + 6):
             tick(s)

@@ -19,6 +19,8 @@ FEATS = 512
 OUTS = 512
 PAIR = 2
 HALVES = 2 * GRAPHS
+FOLDED = 3
+UNFOLDED = PACK - FOLDED
 AHEAD = 3
 
 
@@ -27,8 +29,8 @@ def tile_gcnconv_pa_t_kernel(tc, X, W, out):
     with tc.tile_pool(name="const", bufs=1) as const, tc.tile_pool(name="xin", bufs=AHEAD + 3) as xin, tc.tile_pool(
         name="work", bufs=3
     ) as work, tc.tile_pool(name="deep", bufs=6) as deep, tc.tile_pool(name="single", bufs=1) as single, tc.psum_pool(name="ps_d", bufs=1) as ps_d, tc.psum_pool(
-        name="ps_t", bufs=2
-    ) as ps_t, tc.psum_pool(name="ps_h", bufs=3) as ps_h, tc.psum_pool(name="ps_o", bufs=2) as ps_o, tc.manual_schedule():
+        name="ps_s", bufs=1
+    ) as ps_s, tc.psum_pool(name="ps_t", bufs=2) as ps_t, tc.psum_pool(name="ps_h", bufs=2) as ps_h, tc.psum_pool(name="ps_o", bufs=2) as ps_o, tc.manual_schedule():
         kept = {}
 
         def load(g, half):
@@ -52,6 +54,9 @@ def tile_gcnconv_pa_t_kernel(tc, X, W, out):
 
         ident_f32 = const.tile([P, P], F32)
         make_identity(nc, ident_f32[:])
+
+        ident_bf = const.tile([P, P], BF16)
+        make_identity(nc, ident_bf[:])
 
         w_codes = const.tile([P, OUTS], U32, align_bytes=64)
         w_scales = const.tile([P, OUTS], U8, align_bytes=64)
@@ -79,21 +84,46 @@ def tile_gcnconv_pa_t_kernel(tc, X, W, out):
             nc.vector.quantize_mx(out=codes[:].bitcast(FP8X4), scales=scales[:], in_=grouped)
             return codes, scales
 
+        def fold(g, half):
+            if half == 0:
+                kept[("sums", g)] = ps_s.tile([P, FOLDED, P], F32, name="sums")
+            for j in range(half * PAIR, (half + 1) * PAIR):
+                if j >= UNFOLDED:
+                    for k in range(PACK):
+                        nc.tensor.matmul(
+                            kept[("sums", g)][:, j - UNFOLDED, :],
+                            ident_bf[:],
+                            kept[("a_sb", g)][:, j, k * P : (k + 1) * P],
+                            start=(k == 0),
+                            stop=(k == PACK - 1),
+                        )
+
         def degrees(g, half):
             if half == 0:
                 kept[("deg", g)] = work.tile([P, PACK], F32, name="deg")
+                for j in range(UNFOLDED):
+                    unused = work.tile([P, NODES], BF16, name="unused")
+                    nc.vector.tensor_scalar(
+                        out=unused[:],
+                        in0=kept[("a_sb", g)][:, j, :],
+                        scalar1=1.0,
+                        scalar2=None,
+                        op0=ALU.mult,
+                        op1=ALU.add,
+                        accum_out=kept[("deg", g)][:, j : j + 1],
+                    )
+            else:
+                nc.vector.tensor_reduce(
+                    out=kept[("deg", g)][:, UNFOLDED:PACK],
+                    in_=kept[("sums", g)][:],
+                    axis=mybir.AxisListType.X,
+                    op=ALU.add,
+                )
+
+        def add_identity(g, half):
+            if half == 0:
                 kept[("a_plus_i", g)] = deep.tile([P, PACK, P], F32, name="a_plus_i")
             for j in range(half * PAIR, (half + 1) * PAIR):
-                unused = work.tile([P, NODES], BF16, name="unused")
-                nc.vector.tensor_scalar(
-                    out=unused[:],
-                    in0=kept[("a_sb", g)][:, j, :],
-                    scalar1=1.0,
-                    scalar2=None,
-                    op0=ALU.mult,
-                    op1=ALU.add,
-                    accum_out=kept[("deg", g)][:, j : j + 1],
-                )
                 nc.gpsimd.tensor_tensor(
                     out=kept[("a_plus_i", g)][:, j, :],
                     in0=kept[("a_sb", g)][:, j, j * P : (j + 1) * P],
@@ -257,6 +287,7 @@ def tile_gcnconv_pa_t_kernel(tc, X, W, out):
             at(s - 5, quantise_a)
             at(s - 6, quantise_h)
             at(s - 3, quantise_feat)
+            at(s, fold)
             at(s - 4, transpose)
             if even:
                 take_roots(g_d)
@@ -267,11 +298,12 @@ def tile_gcnconv_pa_t_kernel(tc, X, W, out):
             for a in range(PAIR):
                 at(s - 6, lambda g, half: second_product(g, half, a, draining and a == 1))
             at(s - 6, store)
+            at(s, degrees)
             at(s - 3, normalise)
             if even:
                 inverse_roots(g_d)
             at(s - 2, regroup_feat)
-            at(s, degrees)
+            at(s, add_identity)
 
         for s in range(HALVES + 6):
             tick(s)

@@ -35,7 +35,7 @@ def tile_gcnconv_pa_t_kernel(tc, X, W, out):
 
         def load(g, half):
             if half == 0:
-                kept[("a_sb", g)] = xin.tile([P, PACK, NODES], BF16, name="a_sb")
+                kept[("a_sb", g)] = xin.tile([P, PACK + 1, NODES], BF16, name="a_sb")
                 kept[("f_sb", g)] = xin.tile([P, PACK, FEATS], BF16, name="f_sb")
             slots = slice(half * PAIR, (half + 1) * PAIR)
             rows = slice(half * PAIR * P, (half + 1) * PAIR * P)
@@ -55,6 +55,9 @@ def tile_gcnconv_pa_t_kernel(tc, X, W, out):
         ident_f32 = const.tile([P, P], F32)
         make_identity(nc, ident_f32[:])
 
+        ident_pair = const.tile([P, PAIR, P], F32)
+        for a in range(PAIR):
+            make_identity(nc, ident_pair[:, a, :])
         ident_bf = const.tile([P, P], BF16)
         make_identity(nc, ident_bf[:])
 
@@ -123,13 +126,14 @@ def tile_gcnconv_pa_t_kernel(tc, X, W, out):
         def add_identity(g, half):
             if half == 0:
                 kept[("a_plus_i", g)] = deep.tile([P, PACK, P], F32, name="a_plus_i")
-            for j in range(half * PAIR, (half + 1) * PAIR):
-                nc.gpsimd.tensor_tensor(
-                    out=kept[("a_plus_i", g)][:, j, :],
-                    in0=kept[("a_sb", g)][:, j, j * P : (j + 1) * P],
-                    in1=ident_f32[:],
-                    op=ALU.add,
-                )
+            blocks = kept[("a_sb", g)][:].rearrange("p j m -> p (j m)").rearrange("p (j w) -> p j w", w=NODES + P)
+            slots = slice(half * PAIR, (half + 1) * PAIR)
+            nc.vector.tensor_tensor(
+                out=kept[("a_plus_i", g)][:, slots, :],
+                in0=blocks[:, slots, 0:P],
+                in1=ident_pair[:],
+                op=ALU.add,
+            )
 
         def roots(g):
             deg = kept[("deg", g)]
@@ -284,6 +288,7 @@ def tile_gcnconv_pa_t_kernel(tc, X, W, out):
                 roots(g_d)
             if odd:
                 mask_roots(g_d)
+            at(s - 2, add_identity)
             at(s - 5, quantise_a)
             at(s - 6, quantise_h)
             at(s - 3, quantise_feat)
@@ -303,7 +308,6 @@ def tile_gcnconv_pa_t_kernel(tc, X, W, out):
             if even:
                 inverse_roots(g_d)
             at(s - 2, regroup_feat)
-            at(s, add_identity)
 
         for s in range(HALVES + 6):
             tick(s)

@@ -21,6 +21,11 @@ PAIR = 2
 HALVES = 2 * GRAPHS
 FOLDED = 3
 UNFOLDED = PACK - FOLDED
+H_TICK = HALVES + 3
+O_TICK = HALVES + 4
+LEAST_NORMAL = 2.0**-126
+W_PIECES = 4
+PIECE = 64
 AHEAD = 3
 
 
@@ -28,29 +33,44 @@ def tile_gcnconv_pa_t_kernel(tc, X, W, out):
     nc = tc.nc
     with tc.tile_pool(name="const", bufs=1) as const, tc.tile_pool(name="xin", bufs=AHEAD + 3) as xin, tc.tile_pool(
         name="work", bufs=3
-    ) as work, tc.tile_pool(name="deep", bufs=6) as deep, tc.tile_pool(name="single", bufs=1) as single, tc.psum_pool(name="ps_d", bufs=1) as ps_d, tc.psum_pool(
+    ) as work, tc.tile_pool(name="deep", bufs=6) as deep, tc.tile_pool(name="triple", bufs=3) as triple, tc.psum_pool(name="ps_d", bufs=1) as ps_d, tc.psum_pool(
         name="ps_s", bufs=1
     ) as ps_s, tc.psum_pool(name="ps_t", bufs=2) as ps_t, tc.psum_pool(name="ps_h", bufs=2) as ps_h, tc.psum_pool(name="ps_o", bufs=2) as ps_o, tc.manual_schedule():
         kept = {}
 
+        def load_a(g):
+            kept[("a_sb", g)] = xin.tile([P, PACK + 1, NODES], BF16, name="a_sb")
+            for half in range(2):
+                slots = slice(half * PAIR, (half + 1) * PAIR)
+                rows = slice(half * PAIR * P, (half + 1) * PAIR * P)
+                nc.sync.dma_start(
+                    out=kept[("a_sb", g)][:, slots, :], in_=X[g, rows, 0:NODES].rearrange("(j p) m -> p j m", j=PAIR)
+                )
+
+        def load_f(g):
+            kept[("f_sb", g)] = xin.tile([P, PACK, FEATS], BF16, name="f_sb")
+            for half in range(2):
+                slots = slice(half * PAIR, (half + 1) * PAIR)
+                rows = slice(half * PAIR * P, (half + 1) * PAIR * P)
+                nc.sync.dma_start(
+                    out=kept[("f_sb", g)][:, slots, :], in_=X[g, rows, NODES:].rearrange("(p e) c -> p e c", e=PAIR)
+                )
+
         def load(g, half):
             if half == 0:
-                kept[("a_sb", g)] = xin.tile([P, PACK + 1, NODES], BF16, name="a_sb")
-                kept[("f_sb", g)] = xin.tile([P, PACK, FEATS], BF16, name="f_sb")
-            slots = slice(half * PAIR, (half + 1) * PAIR)
-            rows = slice(half * PAIR * P, (half + 1) * PAIR * P)
-            nc.sync.dma_start(
-                out=kept[("a_sb", g)][:, slots, :], in_=X[g, rows, 0:NODES].rearrange("(j p) m -> p j m", j=PAIR)
-            )
-            nc.sync.dma_start(
-                out=kept[("f_sb", g)][:, slots, :], in_=X[g, rows, NODES:].rearrange("(p e) c -> p e c", e=PAIR)
-            )
+                load_a(g)
+            else:
+                load_f(g)
 
         w_rows = const.tile([P, PACK, OUTS], BF16)
-        for u in range(2 * AHEAD):
-            load(u // 2, u % 2)
-            if u == 1:
-                nc.sync.dma_start(out=w_rows[:], in_=W.rearrange("(t p) o -> p t o", p=P))
+        load_a(0)
+        load_a(1)
+        nc.sync.dma_start(out=w_rows[:], in_=W.rearrange("(t p) o -> p t o", p=P))
+        load_f(0)
+        for g in range(2, AHEAD):
+            load_a(g)
+            load_f(g - 1)
+        load_f(AHEAD - 1)
 
         ident_f32 = const.tile([P, P], F32)
         make_identity(nc, ident_f32[:])
@@ -58,6 +78,8 @@ def tile_gcnconv_pa_t_kernel(tc, X, W, out):
         ident_pair = const.tile([P, PAIR, P], F32)
         for a in range(PAIR):
             make_identity(nc, ident_pair[:, a, :])
+        tiny = const.tile([P, 1], F32)
+        nc.vector.memset(tiny[:], LEAST_NORMAL)
         ident_bf = const.tile([P, P], BF16)
         make_identity(nc, ident_bf[:])
 
@@ -67,14 +89,9 @@ def tile_gcnconv_pa_t_kernel(tc, X, W, out):
         w_grouped = const.tile([P, OUTS, PACK], BF16, align_bytes=64)
 
         def regroup_w():
-            nc.gpsimd.tensor_scalar(
-                out=w_grouped[:],
-                in0=w_rows[:].rearrange("p t o -> p o t"),
-                scalar1=1.0,
-                scalar2=0.0,
-                op0=ALU.mult,
-                op1=ALU.add,
-            )
+            for q in range(W_PIECES):
+                cols = slice(q * (OUTS // W_PIECES), (q + 1) * (OUTS // W_PIECES))
+                nc.scalar.copy(out=w_grouped[:, cols, :], in_=w_rows[:, :, cols].rearrange("p t o -> p o t"))
 
         def quantise_w():
             nc.vector.quantize_mx(
@@ -87,41 +104,38 @@ def tile_gcnconv_pa_t_kernel(tc, X, W, out):
             nc.vector.quantize_mx(out=codes[:].bitcast(FP8X4), scales=scales[:], in_=grouped)
             return codes, scales
 
-        def fold(g, half):
-            if half == 0:
-                kept[("sums", g)] = ps_s.tile([P, FOLDED, P], F32, name="sums")
-            for j in range(half * PAIR, (half + 1) * PAIR):
-                if j >= UNFOLDED:
-                    for k in range(PACK):
-                        nc.tensor.matmul(
-                            kept[("sums", g)][:, j - UNFOLDED, :],
-                            ident_bf[:],
-                            kept[("a_sb", g)][:, j, k * P : (k + 1) * P],
-                            start=(k == 0),
-                            stop=(k == PACK - 1),
-                        )
-
-        def degrees(g, half):
-            if half == 0:
-                kept[("deg", g)] = work.tile([P, PACK], F32, name="deg")
-                for j in range(UNFOLDED):
-                    unused = work.tile([P, NODES], BF16, name="unused")
-                    nc.vector.tensor_scalar(
-                        out=unused[:],
-                        in0=kept[("a_sb", g)][:, j, :],
-                        scalar1=1.0,
-                        scalar2=None,
-                        op0=ALU.mult,
-                        op1=ALU.add,
-                        accum_out=kept[("deg", g)][:, j : j + 1],
-                    )
-            else:
-                nc.vector.tensor_reduce(
-                    out=kept[("deg", g)][:, UNFOLDED:PACK],
-                    in_=kept[("sums", g)][:],
-                    axis=mybir.AxisListType.X,
-                    op=ALU.add,
+        def fold(g):
+            kept[("sums", g)] = ps_s.tile([P, FOLDED, PIECE], F32, name="sums")
+            for k in range(NODES // PIECE):
+                nc.tensor.matmul(
+                    kept[("sums", g)][:],
+                    ident_bf[:],
+                    kept[("a_sb", g)][:, UNFOLDED:PACK, k * PIECE : (k + 1) * PIECE],
+                    start=(k == 0),
+                    stop=(k == NODES // PIECE - 1),
                 )
+
+        def sum_tile(g):
+            kept[("deg", g)] = work.tile([P, PACK], F32, name="deg")
+            for j in range(UNFOLDED):
+                unused = work.tile([P, NODES], BF16, name="unused")
+                nc.vector.tensor_scalar(
+                    out=unused[:],
+                    in0=kept[("a_sb", g)][:, j, :],
+                    scalar1=1.0,
+                    scalar2=None,
+                    op0=ALU.mult,
+                    op1=ALU.add,
+                    accum_out=kept[("deg", g)][:, j : j + 1],
+                )
+
+        def sum_folded(g):
+            nc.vector.tensor_reduce(
+                out=kept[("deg", g)][:, UNFOLDED:PACK],
+                in_=kept[("sums", g)][:],
+                axis=mybir.AxisListType.X,
+                op=ALU.add,
+            )
 
         def add_identity(g, half):
             if half == 0:
@@ -129,23 +143,12 @@ def tile_gcnconv_pa_t_kernel(tc, X, W, out):
             blocks = kept[("a_sb", g)][:].rearrange("p j m -> p (j m)").rearrange("p (j w) -> p j w", w=NODES + P)
             slots = slice(half * PAIR, (half + 1) * PAIR)
             nc.vector.tensor_tensor(
-                out=kept[("a_plus_i", g)][:, slots, :],
-                in0=blocks[:, slots, 0:P],
-                in1=ident_pair[:],
-                op=ALU.add,
+                out=kept[("a_plus_i", g)][:, slots, :], in0=blocks[:, slots, 0:P], in1=ident_pair[:], op=ALU.add
             )
 
         def roots(g):
-            deg = kept[("deg", g)]
-            safe = work.tile([P, PACK], F32, name="safe")
-            nc.vector.scalar_tensor_tensor(
-                out=safe[:], in0=deg[:], scalar=0.0, in1=deg[:], op0=ALU.is_le, op1=ALU.max
-            )
-            kept[("safe", g)] = safe
-
-        def take_roots(g):
             root = work.tile([P, PACK], F32, name="root")
-            nc.scalar.sqrt(root[:], kept[("safe", g)][:])
+            nc.scalar.activation(out=root[:], in_=kept[("deg", g)][:], func=ACT.Sqrt, bias=tiny[:])
             kept[("root", g)] = root
 
         def inverse_roots(g):
@@ -168,7 +171,7 @@ def tile_gcnconv_pa_t_kernel(tc, X, W, out):
             kept[("d_free", g)] = d_free
 
         def regroup_feat(g, half):
-            f_grouped = single.tile([P, FEATS // 2, PACK], BF16, align_bytes=64, name="f_grouped")
+            f_grouped = triple.tile([P, FEATS // 2, PACK], BF16, align_bytes=64, name="f_grouped")
             first = half * (FEATS // 2)
             nc.gpsimd.tensor_scalar(
                 out=f_grouped[:],
@@ -227,7 +230,7 @@ def tile_gcnconv_pa_t_kernel(tc, X, W, out):
             kept[("a", g, half)] = quantise(work, kept[("a_grouped", g, half)][:].rearrange("p a n t -> p (a n t)"), "a")
             kept[("h_grouped", g, half)] = work.tile([P, PAIR, P, PACK], BF16, align_bytes=64, name="h_grouped")
 
-        def first_product(g, half, a, on_vector):
+        def first_product(g, half, a):
             a_codes, a_scales = kept[("a", g, half)]
             h_t = ps_h.tile([P, PACK, P], F32, name="h_t")
             for t in range(PACK):
@@ -242,18 +245,19 @@ def tile_gcnconv_pa_t_kernel(tc, X, W, out):
                     start=True,
                     stop=True,
                 )
-            if on_vector:
-                nc.vector.tensor_copy(
-                    out=kept[("h_grouped", g, half)][:, a, :, :], in_=h_t[:].rearrange("p t n -> p n t")
-                )
-            else:
-                nc.scalar.copy(out=kept[("h_grouped", g, half)][:, a, :, :], in_=h_t[:].rearrange("p t n -> p n t"))
+            kept[("h_t", g, half, a)] = h_t
+
+        def copy_h(g, half, a, engine_copy):
+            engine_copy(
+                out=kept[("h_grouped", g, half)][:, a, :, :],
+                in_=kept[("h_t", g, half, a)][:].rearrange("p t n -> p n t"),
+            )
 
         def quantise_h(g, half):
             kept[("h", g, half)] = quantise(work, kept[("h_grouped", g, half)][:].rearrange("p a n t -> p (a n t)"), "h")
             kept[("result", g, half)] = work.tile([P, PAIR, OUTS], F32, name="result")
 
-        def second_product(g, half, a, on_vector):
+        def second_product(g, half, a):
             h_codes, h_scales = kept[("h", g, half)]
             o_ps = ps_o.tile([P, OUTS], F32, name="o_ps")
             nc.tensor.matmul_mx(
@@ -265,10 +269,15 @@ def tile_gcnconv_pa_t_kernel(tc, X, W, out):
                 start=True,
                 stop=True,
             )
+            kept[("o_ps", g, half, a)] = o_ps
+
+        def relu(g, half, a, on_vector):
+            result = kept[("result", g, half)][:, a, :]
+            o_ps = kept[("o_ps", g, half, a)]
             if on_vector:
-                nc.vector.tensor_scalar_max(out=kept[("result", g, half)][:, a, :], in0=o_ps[:], scalar1=0.0)
+                nc.vector.tensor_scalar_max(out=result, in0=o_ps[:], scalar1=0.0)
             else:
-                nc.scalar.activation(out=kept[("result", g, half)][:, a, :], in_=o_ps[:], func=ACT.Relu)
+                nc.scalar.activation(out=result, in_=o_ps[:], func=ACT.Relu)
 
         def store(g, half):
             out_rows = out[g].rearrange("(j p) o -> p j o", j=PACK)
@@ -279,39 +288,77 @@ def tile_gcnconv_pa_t_kernel(tc, X, W, out):
                 stage(u // 2, u % 2)
 
         def tick(s):
-            draining = s - 3 >= HALVES
-            at(s + 2 * AHEAD, load)
+            filling = s < 5
+            even = s % 2 == 0
             g_d = s // 2 - 1
-            even = s % 2 == 0 and 0 <= g_d < GRAPHS
-            odd = s % 2 == 1 and 0 <= g_d < GRAPHS
-            if even:
-                roots(g_d)
-            if odd:
-                mask_roots(g_d)
-            at(s - 2, add_identity)
+
+            def for_graph(g, *stages):
+                if 0 <= g < GRAPHS:
+                    for stage in stages:
+                        stage(g)
+
+            at(s + 2 * AHEAD, load)
+
+            if filling and even:
+                at(s - 3, normalise)
+            if s == 2:
+                for u in range(4):
+                    at(u, add_identity)
+            if not even:
+                for_graph(g_d, mask_roots)
+            if s >= 4:
+                at(s, add_identity)
             at(s - 5, quantise_a)
             at(s - 6, quantise_h)
-            at(s - 3, quantise_feat)
-            at(s, fold)
+            if s == 6:
+                quantise_w()
+            if s == 5:
+                at(0, quantise_feat)
+            if not filling:
+                at(s - 4, quantise_feat)
+
+            at(s - 2, regroup_feat)
+
             at(s - 4, transpose)
             if even:
-                take_roots(g_d)
-            if odd:
-                spread(g_d)
+                if s == 0 or s == 4:
+                    for_graph(s // 2, fold)
+            else:
+                for_graph(s // 2, roots)
+                for_graph(g_d, spread)
+            h_on_vector = s >= H_TICK
+            o_on_vector = s >= O_TICK
             for a in range(PAIR):
-                at(s - 5, lambda g, half: first_product(g, half, a, draining and a == 1))
+                at(s - 5, lambda g, half: first_product(g, half, a))
+                if not (h_on_vector and a == 1):
+                    at(s - 5, lambda g, half: copy_h(g, half, a, nc.scalar.copy))
             for a in range(PAIR):
-                at(s - 6, lambda g, half: second_product(g, half, a, draining and a == 1))
-            at(s - 6, store)
-            at(s, degrees)
-            at(s - 3, normalise)
+                at(s - 6, lambda g, half: second_product(g, half, a))
+                if not (o_on_vector and a == 1):
+                    at(s - 6, lambda g, half: relu(g, half, a, False))
+            if not even and s != 3:
+                for_graph(s // 2 + 1, fold)
+
+            if s == 0:
+                for_graph(0, sum_tile)
             if even:
-                inverse_roots(g_d)
-            at(s - 2, regroup_feat)
+                for_graph(s // 2, *([] if filling and s else [sum_folded]))
+                for_graph(g_d, inverse_roots)
+                if filling and s:
+                    for_graph(s // 2, sum_folded)
+            elif not filling:
+                for_graph(s // 2 + 1, sum_tile)
+            if not (filling and even):
+                at(s - 3, normalise)
+            if filling and not even:
+                for_graph(s // 2 + 1, sum_tile)
+            if h_on_vector:
+                at(s - 5, lambda g, half: copy_h(g, half, 1, nc.vector.tensor_copy))
+            if o_on_vector:
+                at(s - 6, lambda g, half: relu(g, half, 1, True))
+            at(s - 6, store)
 
         for s in range(HALVES + 6):
             tick(s)
             if s == 2:
                 regroup_w()
-            if s == 5:
-                quantise_w()

@@ -22,7 +22,7 @@ HALVES = 2 * GRAPHS
 FOLDED = 3
 UNFOLDED = PACK - FOLDED
 H_TICK = HALVES + 3
-O_TICK = HALVES + 4
+O_TICK = HALVES + 5
 LEAST_NORMAL = 2.0**-126
 W_PIECES = 4
 PIECE = 64
@@ -290,32 +290,28 @@ def tile_gcnconv_pa_t_kernel(tc, X, W, out):
         def tick(s):
             filling = s < 5
             even = s % 2 == 0
-            g_d = s // 2 - 1
 
-            def for_graph(g, *stages):
+            def for_graph(g, stage):
                 if 0 <= g < GRAPHS:
-                    for stage in stages:
-                        stage(g)
+                    stage(g)
 
             at(s + 2 * AHEAD, load)
 
-            if filling and even:
+            early = even and s < 7
+            if early:
                 at(s - 3, normalise)
-            if s == 2:
-                for u in range(4):
-                    at(u, add_identity)
-            if not even:
-                for_graph(g_d, mask_roots)
             if s >= 4:
                 at(s, add_identity)
             at(s - 5, quantise_a)
-            at(s - 6, quantise_h)
             if s == 6:
                 quantise_w()
             if s == 5:
                 at(0, quantise_feat)
             if not filling:
                 at(s - 4, quantise_feat)
+            at(s - 6, quantise_h)
+            if even:
+                for_graph(s // 2 - 1, mask_roots)
 
             at(s - 2, regroup_feat)
 
@@ -324,8 +320,7 @@ def tile_gcnconv_pa_t_kernel(tc, X, W, out):
                 if s == 0 or s == 4:
                     for_graph(s // 2, fold)
             else:
-                for_graph(s // 2, roots)
-                for_graph(g_d, spread)
+                for_graph(s // 2 - 1, spread)
             h_on_vector = s >= H_TICK
             o_on_vector = s >= O_TICK
             for a in range(PAIR):
@@ -342,16 +337,23 @@ def tile_gcnconv_pa_t_kernel(tc, X, W, out):
             if s == 0:
                 for_graph(0, sum_tile)
             if even:
-                for_graph(s // 2, *([] if filling and s else [sum_folded]))
-                for_graph(g_d, inverse_roots)
-                if filling and s:
-                    for_graph(s // 2, sum_folded)
+                for_graph(s // 2, sum_folded)
+                for_graph(s // 2, roots)
             elif not filling:
                 for_graph(s // 2 + 1, sum_tile)
-            if not (filling and even):
+            if not early:
                 at(s - 3, normalise)
             if filling and not even:
                 for_graph(s // 2 + 1, sum_tile)
+            if s == 1:
+                at(0, add_identity)
+            if not even:
+                for_graph(s // 2, inverse_roots)
+            if s == 1:
+                at(1, add_identity)
+            if s == 2:
+                at(2, add_identity)
+                at(3, add_identity)
             if h_on_vector:
                 at(s - 5, lambda g, half: copy_h(g, half, 1, nc.vector.tensor_copy))
             if o_on_vector:
@@ -360,5 +362,5 @@ def tile_gcnconv_pa_t_kernel(tc, X, W, out):
 
         for s in range(HALVES + 6):
             tick(s)
-            if s == 2:
+            if s == 1:
                 regroup_w()

@@ -21,11 +21,11 @@ PAIR = 2
 HALVES = 2 * GRAPHS
 FOLDED = 3
 UNFOLDED = PACK - FOLDED
-H_TICK = HALVES + 3
-O_TICK = HALVES + 5
+H_TICK = HALVES + 2
+O_TICK = HALVES + 4
 LEAST_NORMAL = 2.0**-126
 W_PIECES = 4
-PIECE = 64
+PIECE = 32
 AHEAD = 3
 
 
@@ -33,9 +33,9 @@ def tile_gcnconv_pa_t_kernel(tc, X, W, out):
     nc = tc.nc
     with tc.tile_pool(name="const", bufs=1) as const, tc.tile_pool(name="xin", bufs=AHEAD + 3) as xin, tc.tile_pool(
         name="work", bufs=3
-    ) as work, tc.tile_pool(name="deep", bufs=6) as deep, tc.tile_pool(name="triple", bufs=3) as triple, tc.psum_pool(name="ps_d", bufs=1) as ps_d, tc.psum_pool(
+    ) as work, tc.tile_pool(name="deep", bufs=6) as deep, tc.tile_pool(name="double", bufs=2) as double, tc.psum_pool(name="ps_d", bufs=1) as ps_d, tc.psum_pool(
         name="ps_s", bufs=1
-    ) as ps_s, tc.psum_pool(name="ps_t", bufs=2) as ps_t, tc.psum_pool(name="ps_h", bufs=2) as ps_h, tc.psum_pool(name="ps_o", bufs=2) as ps_o, tc.manual_schedule():
+    ) as ps_s, tc.psum_pool(name="ps_i", bufs=1) as ps_i, tc.psum_pool(name="ps_t", bufs=1) as ps_t, tc.psum_pool(name="ps_h", bufs=2) as ps_h, tc.psum_pool(name="ps_o", bufs=2) as ps_o, tc.manual_schedule():
         kept = {}
 
         def load_a(g):
@@ -75,9 +75,9 @@ def tile_gcnconv_pa_t_kernel(tc, X, W, out):
         ident_f32 = const.tile([P, P], F32)
         make_identity(nc, ident_f32[:])
 
-        ident_pair = const.tile([P, PAIR, P], F32)
+        ident_pair = ps_i.tile([P, PAIR, P], F32)
         for a in range(PAIR):
-            make_identity(nc, ident_pair[:, a, :])
+            nc.tensor.transpose(ident_pair[:, a, :], ident_f32[:], ident_f32[:])
         tiny = const.tile([P, 1], F32)
         nc.vector.memset(tiny[:], LEAST_NORMAL)
         ident_bf = const.tile([P, P], BF16)
@@ -98,11 +98,21 @@ def tile_gcnconv_pa_t_kernel(tc, X, W, out):
                 out=w_codes[:].bitcast(FP8X4), scales=w_scales[:], in_=w_grouped[:].rearrange("p o t -> p (o t)")
             )
 
-        def quantise(pool, grouped, name):
+        def quantise(pool, grouped, name, parts=1):
             codes = pool.tile([P, PAIR * P], U32, align_bytes=64, name=name + "_codes")
             scales = pool.tile([P, PAIR * P], U8, align_bytes=64, name=name + "_scales")
-            nc.vector.quantize_mx(out=codes[:].bitcast(FP8X4), scales=scales[:], in_=grouped)
+            width = PAIR * P // parts
+            for part in range(parts):
+                cols = slice(part * width, (part + 1) * width)
+                nc.vector.quantize_mx(
+                    out=codes[:, cols].bitcast(FP8X4),
+                    scales=scales[:, cols],
+                    in_=grouped[:, part * width * PACK : (part + 1) * width * PACK],
+                )
             return codes, scales
+
+        def tiles_apart(g, half):
+            return PAIR if g == GRAPHS - 1 and half == 1 else 1
 
         def fold(g):
             kept[("sums", g)] = ps_s.tile([P, FOLDED, PIECE], F32, name="sums")
@@ -115,9 +125,9 @@ def tile_gcnconv_pa_t_kernel(tc, X, W, out):
                     stop=(k == NODES // PIECE - 1),
                 )
 
-        def sum_tile(g):
+        def sum_tiles(g, tiles):
             kept[("deg", g)] = work.tile([P, PACK], F32, name="deg")
-            for j in range(UNFOLDED):
+            for j in tiles:
                 unused = work.tile([P, NODES], BF16, name="unused")
                 nc.vector.tensor_scalar(
                     out=unused[:],
@@ -128,6 +138,9 @@ def tile_gcnconv_pa_t_kernel(tc, X, W, out):
                     op1=ALU.add,
                     accum_out=kept[("deg", g)][:, j : j + 1],
                 )
+
+        def sum_tile(g):
+            sum_tiles(g, range(UNFOLDED))
 
         def sum_folded(g):
             nc.vector.tensor_reduce(
@@ -171,7 +184,7 @@ def tile_gcnconv_pa_t_kernel(tc, X, W, out):
             kept[("d_free", g)] = d_free
 
         def regroup_feat(g, half):
-            f_grouped = triple.tile([P, FEATS // 2, PACK], BF16, align_bytes=64, name="f_grouped")
+            f_grouped = double.tile([P, FEATS // 2, PACK], BF16, align_bytes=64, name="f_grouped")
             first = half * (FEATS // 2)
             nc.gpsimd.tensor_scalar(
                 out=f_grouped[:],
@@ -217,17 +230,19 @@ def tile_gcnconv_pa_t_kernel(tc, X, W, out):
                     first = (2 * a + u) * P
                     nc.tensor.transpose(a_t[:, a, u, :], words[:, first : first + P], ident_f32[:])
             a_grouped = work.tile([P, PAIR, P, PACK], BF16, align_bytes=64, name="a_grouped")
-            nc.scalar.copy(
-                out=a_grouped[:]
-                .rearrange("p a n t -> p (a n t)")
-                .bitcast(F32)
-                .rearrange("p (a n u) -> p a n u", a=PAIR, u=2),
-                in_=a_t[:].rearrange("p a u n -> p a n u"),
+            out_words = (
+                a_grouped[:].rearrange("p a n t -> p (a n t)").bitcast(F32).rearrange("p (a n u) -> p a n u", a=PAIR, u=2)
             )
+            in_words = a_t[:].rearrange("p a u n -> p a n u")
+            if tiles_apart(g, half) == 1:
+                nc.scalar.copy(out=out_words, in_=in_words)
+            else:
+                nc.scalar.copy(out=out_words[:, 0, :, :], in_=in_words[:, 0, :, :])
+                nc.vector.tensor_copy(out=out_words[:, 1, :, :], in_=in_words[:, 1, :, :])
             kept[("a_grouped", g, half)] = a_grouped
 
         def quantise_a(g, half):
-            kept[("a", g, half)] = quantise(work, kept[("a_grouped", g, half)][:].rearrange("p a n t -> p (a n t)"), "a")
+            kept[("a", g, half)] = quantise(work, kept[("a_grouped", g, half)][:].rearrange("p a n t -> p (a n t)"), "a", tiles_apart(g, half))
             kept[("h_grouped", g, half)] = work.tile([P, PAIR, P, PACK], BF16, align_bytes=64, name="h_grouped")
 
         def first_product(g, half, a):
@@ -254,7 +269,7 @@ def tile_gcnconv_pa_t_kernel(tc, X, W, out):
             )
 
         def quantise_h(g, half):
-            kept[("h", g, half)] = quantise(work, kept[("h_grouped", g, half)][:].rearrange("p a n t -> p (a n t)"), "h")
+            kept[("h", g, half)] = quantise(work, kept[("h_grouped", g, half)][:].rearrange("p a n t -> p (a n t)"), "h", tiles_apart(g, half))
             kept[("result", g, half)] = work.tile([P, PAIR, OUTS], F32, name="result")
 
         def second_product(g, half, a):
@@ -281,15 +296,27 @@ def tile_gcnconv_pa_t_kernel(tc, X, W, out):
 
         def store(g, half):
             out_rows = out[g].rearrange("(j p) o -> p j o", j=PACK)
-            nc.sync.dma_start(out=out_rows[:, half * PAIR : (half + 1) * PAIR, :], in_=kept[("result", g, half)][:])
+            apart = tiles_apart(g, half)
+            for part in range(apart):
+                first, n = part * PAIR // apart, PAIR // apart
+                nc.sync.dma_start(
+                    out=out_rows[:, half * PAIR + first : half * PAIR + first + n, :],
+                    in_=kept[("result", g, half)][:, first : first + n, :],
+                )
 
         def at(u, stage):
             if 0 <= u < HALVES:
                 stage(u // 2, u % 2)
 
         def tick(s):
-            filling = s < 5
+            k = s // 2
             even = s % 2 == 0
+            def h_on_vector(s):
+                return s >= H_TICK
+
+            def o_on_vector(s):
+                return s >= O_TICK
+
 
             def for_graph(g, stage):
                 if 0 <= g < GRAPHS:
@@ -297,68 +324,68 @@ def tile_gcnconv_pa_t_kernel(tc, X, W, out):
 
             at(s + 2 * AHEAD, load)
 
-            early = even and s < 7
-            if early:
-                at(s - 3, normalise)
+            if s == 0:
+                sum_tiles(0, range(PACK))
+            if even and s and s != 4:
+                for_graph(k, sum_folded)
+            if not even and s != 3:
+                for_graph(k + 1, sum_tile)
+            at(s - 3, normalise)
+            if s == 3:
+                for_graph(k + 1, sum_tile)
+            if s == 4:
+                for_graph(k, sum_folded)
             if s >= 4:
                 at(s, add_identity)
-            at(s - 5, quantise_a)
-            if s == 6:
-                quantise_w()
-            if s == 5:
-                at(0, quantise_feat)
-            if not filling:
-                at(s - 4, quantise_feat)
-            at(s - 6, quantise_h)
-            if even:
-                for_graph(s // 2 - 1, mask_roots)
-
-            at(s - 2, regroup_feat)
-
-            at(s - 4, transpose)
-            if even:
-                if s == 0 or s == 4:
-                    for_graph(s // 2, fold)
-            else:
-                for_graph(s // 2 - 1, spread)
-            h_on_vector = s >= H_TICK
-            o_on_vector = s >= O_TICK
-            for a in range(PAIR):
-                at(s - 5, lambda g, half: first_product(g, half, a))
-                if not (h_on_vector and a == 1):
-                    at(s - 5, lambda g, half: copy_h(g, half, a, nc.scalar.copy))
-            for a in range(PAIR):
-                at(s - 6, lambda g, half: second_product(g, half, a))
-                if not (o_on_vector and a == 1):
-                    at(s - 6, lambda g, half: relu(g, half, a, False))
-            if not even and s != 3:
-                for_graph(s // 2 + 1, fold)
-
-            if s == 0:
-                for_graph(0, sum_tile)
-            if even:
-                for_graph(s // 2, sum_folded)
-                for_graph(s // 2, roots)
-            elif not filling:
-                for_graph(s // 2 + 1, sum_tile)
-            if not early:
-                at(s - 3, normalise)
-            if filling and not even:
-                for_graph(s // 2 + 1, sum_tile)
+            if h_on_vector(s - 1):
+                at(s - 5, lambda g, half: copy_h(g, half, 1, nc.vector.tensor_copy))
+            if o_on_vector(s - 1):
+                at(s - 6, lambda g, half: relu(g, half, 1, True))
+                at(s - 6, store)
             if s == 1:
                 at(0, add_identity)
             if not even:
-                for_graph(s // 2, inverse_roots)
+                for_graph(k, inverse_roots)
             if s == 1:
                 at(1, add_identity)
-            if s == 2:
+                mask_roots(0)
                 at(2, add_identity)
                 at(3, add_identity)
-            if h_on_vector:
-                at(s - 5, lambda g, half: copy_h(g, half, 1, nc.vector.tensor_copy))
-            if o_on_vector:
-                at(s - 6, lambda g, half: relu(g, half, 1, True))
-            at(s - 6, store)
+            if s == 4:
+                for_graph(1, mask_roots)
+            at(s - 4, quantise_a)
+            if s == 5:
+                quantise_w()
+            if s == 4:
+                at(0, quantise_feat)
+            if s >= 4:
+                at(s - 3, quantise_feat)
+            at(s - 5, quantise_h)
+            if not even and s > 3:
+                for_graph(k, mask_roots)
+
+            at(s - 2, regroup_feat)
+
+            if even:
+                for_graph(k, roots)
+            if not even and s != 3:
+                for_graph(k + 1, fold)
+            at(s - 3, transpose)
+            if even:
+                for_graph(k - 1, spread)
+            if s == 3:
+                for_graph(k + 1, fold)
+            for a in range(PAIR):
+                at(s - 4, lambda g, half: first_product(g, half, a))
+                if not (h_on_vector(s) and a == 1):
+                    at(s - 4, lambda g, half: copy_h(g, half, a, nc.scalar.copy))
+            for a in range(PAIR):
+                at(s - 5, lambda g, half: second_product(g, half, a))
+                if not (o_on_vector(s) and a == 1):
+                    at(s - 5, lambda g, half: relu(g, half, a, False))
+
+            if not o_on_vector(s):
+                at(s - 5, store)
 
         for s in range(HALVES + 6):
             tick(s)

@@ -22,8 +22,10 @@ HALVES = 2 * GRAPHS
 FOLDED = 3
 UNFOLDED = PACK - FOLDED
 H_TICK = HALVES + 2
-O_TICK = HALVES + 4
+O_TICK = HALVES + 2
 LEAST_NORMAL = 2.0**-126
+RS = (2,)
+F_PIECES = 2
 W_PIECES = 4
 PIECE = 32
 AHEAD = 3
@@ -186,14 +188,20 @@ def tile_gcnconv_pa_t_kernel(tc, X, W, out):
         def regroup_feat(g, half):
             f_grouped = double.tile([P, FEATS // 2, PACK], BF16, align_bytes=64, name="f_grouped")
             first = half * (FEATS // 2)
-            nc.gpsimd.tensor_scalar(
-                out=f_grouped[:],
-                in0=kept[("f_sb", g)][:, :, first : first + FEATS // 2].rearrange("p t c -> p c t"),
-                scalar1=1.0,
-                scalar2=0.0,
-                op0=ALU.mult,
-                op1=ALU.add,
-            )
+            f_columns = kept[("f_sb", g)][:, :, first : first + FEATS // 2].rearrange("p t c -> p c t")
+            if 2 * g + half in RS:
+                nc.scalar.copy(out=f_grouped[:], in_=f_columns)
+            else:
+                n = FEATS // 2 // F_PIECES
+                for i in range(F_PIECES):
+                    nc.gpsimd.tensor_scalar(
+                        out=f_grouped[:, i * n : (i + 1) * n, :],
+                        in0=f_columns[:, i * n : (i + 1) * n, :],
+                        scalar1=1.0,
+                        scalar2=0.0,
+                        op0=ALU.mult,
+                        op1=ALU.add,
+                    )
             kept[("f_grouped", g, half)] = f_grouped
 
         def quantise_feat(g, half):
@@ -335,13 +343,10 @@ def tile_gcnconv_pa_t_kernel(tc, X, W, out):
                 for_graph(k + 1, sum_tile)
             if s == 4:
                 for_graph(k, sum_folded)
-            if s >= 4:
-                at(s, add_identity)
+            if s >= 6:
+                at(s - 2, add_identity)
             if h_on_vector(s - 1):
                 at(s - 5, lambda g, half: copy_h(g, half, 1, nc.vector.tensor_copy))
-            if o_on_vector(s - 1):
-                at(s - 6, lambda g, half: relu(g, half, 1, True))
-                at(s - 6, store)
             if s == 1:
                 at(0, add_identity)
             if not even:
@@ -364,13 +369,20 @@ def tile_gcnconv_pa_t_kernel(tc, X, W, out):
             if not even and s > 3:
                 for_graph(k, mask_roots)
 
-            at(s - 2, regroup_feat)
+            if o_on_vector(s - 1):
+                at(s - 6, lambda g, half: relu(g, half, 1, True))
+                at(s - 6, store)
+
+            if s - 2 not in RS:
+                at(s - 2, regroup_feat)
 
             if even:
                 for_graph(k, roots)
             if not even and s != 3:
                 for_graph(k + 1, fold)
             at(s - 3, transpose)
+            if s - 2 in RS:
+                at(s - 2, regroup_feat)
             if even:
                 for_graph(k - 1, spread)
             if s == 3:

import concourse.mybir as mybir
from concourse.masks import make_identity

FLOPS = 2 * 2 * 16 * 512 * 512 * 512

BF16 = mybir.dt.bfloat16
F32 = mybir.dt.float32
U32 = mybir.dt.uint32
U8 = mybir.dt.uint8
FP8X4 = mybir.dt.float8_e4m3fn_x4
ALU = mybir.AluOpType
ACT = mybir.ActivationFunctionType

P = 128
PACK = 4
GRAPHS = 16
NODES = 512
FEATS = 512
OUTS = 512
PAIR = 2
HALVES = 2 * GRAPHS
FOLDED = 3
UNFOLDED = PACK - FOLDED
H_TICK = HALVES + 2
O_TICK = HALVES + 2
LEAST_NORMAL = 2.0**-126
RS = (2,)
F_PIECES = 2
W_PIECES = 4
PIECE = 32
AHEAD = 3


def tile_gcnconv_pa_t_kernel(tc, X, W, out):
    nc = tc.nc
    with tc.tile_pool(name="const", bufs=1) as const, tc.tile_pool(name="xin", bufs=AHEAD + 3) as xin, tc.tile_pool(
        name="work", bufs=3
    ) as work, tc.tile_pool(name="deep", bufs=6) as deep, tc.tile_pool(name="double", bufs=2) as double, tc.psum_pool(name="ps_d", bufs=1) as ps_d, tc.psum_pool(
        name="ps_s", bufs=1
    ) as ps_s, tc.psum_pool(name="ps_i", bufs=1) as ps_i, tc.psum_pool(name="ps_t", bufs=1) as ps_t, tc.psum_pool(name="ps_h", bufs=2) as ps_h, tc.psum_pool(name="ps_o", bufs=2) as ps_o, tc.manual_schedule():
        kept = {}

        def load_a(g):
            kept[("a_sb", g)] = xin.tile([P, PACK + 1, NODES], BF16, name="a_sb")
            for half in range(2):
                slots = slice(half * PAIR, (half + 1) * PAIR)
                rows = slice(half * PAIR * P, (half + 1) * PAIR * P)
                nc.sync.dma_start(
                    out=kept[("a_sb", g)][:, slots, :], in_=X[g, rows, 0:NODES].rearrange("(j p) m -> p j m", j=PAIR)
                )

        def load_f(g):
            kept[("f_sb", g)] = xin.tile([P, PACK, FEATS], BF16, name="f_sb")
            for half in range(2):
                slots = slice(half * PAIR, (half + 1) * PAIR)
                rows = slice(half * PAIR * P, (half + 1) * PAIR * P)
                nc.sync.dma_start(
                    out=kept[("f_sb", g)][:, slots, :], in_=X[g, rows, NODES:].rearrange("(p e) c -> p e c", e=PAIR)
                )

        def load(g, half):
            if half == 0:
                load_a(g)
            else:
                load_f(g)

        w_rows = const.tile([P, PACK, OUTS], BF16)
        load_a(0)
        load_a(1)
        nc.sync.dma_start(out=w_rows[:], in_=W.rearrange("(t p) o -> p t o", p=P))
        load_f(0)
        for g in range(2, AHEAD):
            load_a(g)
            load_f(g - 1)
        load_f(AHEAD - 1)

        ident_f32 = const.tile([P, P], F32)
        make_identity(nc, ident_f32[:])

        ident_pair = ps_i.tile([P, PAIR, P], F32)
        for a in range(PAIR):
            nc.tensor.transpose(ident_pair[:, a, :], ident_f32[:], ident_f32[:])
        tiny = const.tile([P, 1], F32)
        nc.vector.memset(tiny[:], LEAST_NORMAL)
        ident_bf = const.tile([P, P], BF16)
        make_identity(nc, ident_bf[:])

        w_codes = const.tile([P, OUTS], U32, align_bytes=64)
        w_scales = const.tile([P, OUTS], U8, align_bytes=64)

        w_grouped = const.tile([P, OUTS, PACK], BF16, align_bytes=64)

        def regroup_w():
            for q in range(W_PIECES):
                cols = slice(q * (OUTS // W_PIECES), (q + 1) * (OUTS // W_PIECES))
                nc.scalar.copy(out=w_grouped[:, cols, :], in_=w_rows[:, :, cols].rearrange("p t o -> p o t"))

        def quantise_w():
            nc.vector.quantize_mx(
                out=w_codes[:].bitcast(FP8X4), scales=w_scales[:], in_=w_grouped[:].rearrange("p o t -> p (o t)")
            )

        def quantise(pool, grouped, name, parts=1):
            codes = pool.tile([P, PAIR * P], U32, align_bytes=64, name=name + "_codes")
            scales = pool.tile([P, PAIR * P], U8, align_bytes=64, name=name + "_scales")
            width = PAIR * P // parts
            for part in range(parts):
                cols = slice(part * width, (part + 1) * width)
                nc.vector.quantize_mx(
                    out=codes[:, cols].bitcast(FP8X4),
                    scales=scales[:, cols],
                    in_=grouped[:, part * width * PACK : (part + 1) * width * PACK],
                )
            return codes, scales

        def tiles_apart(g, half):
            return PAIR if g == GRAPHS - 1 and half == 1 else 1

        def fold(g):
            kept[("sums", g)] = ps_s.tile([P, FOLDED, PIECE], F32, name="sums")
            for k in range(NODES // PIECE):
                nc.tensor.matmul(
                    kept[("sums", g)][:],
                    ident_bf[:],
                    kept[("a_sb", g)][:, UNFOLDED:PACK, k * PIECE : (k + 1) * PIECE],
                    start=(k == 0),
                    stop=(k == NODES // PIECE - 1),
                )

        def sum_tiles(g, tiles):
            kept[("deg", g)] = work.tile([P, PACK], F32, name="deg")
            for j in tiles:
                unused = work.tile([P, NODES], BF16, name="unused")
                nc.vector.tensor_scalar(
                    out=unused[:],
                    in0=kept[("a_sb", g)][:, j, :],
                    scalar1=1.0,
                    scalar2=None,
                    op0=ALU.mult,
                    op1=ALU.add,
                    accum_out=kept[("deg", g)][:, j : j + 1],
                )

        def sum_tile(g):
            sum_tiles(g, range(UNFOLDED))

        def sum_folded(g):
            nc.vector.tensor_reduce(
                out=kept[("deg", g)][:, UNFOLDED:PACK],
                in_=kept[("sums", g)][:],
                axis=mybir.AxisListType.X,
                op=ALU.add,
            )

        def add_identity(g, half):
            if half == 0:
                kept[("a_plus_i", g)] = deep.tile([P, PACK, P], F32, name="a_plus_i")
            blocks = kept[("a_sb", g)][:].rearrange("p j m -> p (j m)").rearrange("p (j w) -> p j w", w=NODES + P)
            slots = slice(half * PAIR, (half + 1) * PAIR)
            nc.vector.tensor_tensor(
                out=kept[("a_plus_i", g)][:, slots, :], in0=blocks[:, slots, 0:P], in1=ident_pair[:], op=ALU.add
            )

        def roots(g):
            root = work.tile([P, PACK], F32, name="root")
            nc.scalar.activation(out=root[:], in_=kept[("deg", g)][:], func=ACT.Sqrt, bias=tiny[:])
            kept[("root", g)] = root

        def inverse_roots(g):
            inv = work.tile([P, PACK], F32, name="inv")
            nc.vector.reciprocal(inv[:], kept[("root", g)][:])
            kept[("inv", g)] = inv

        def mask_roots(g):
            d = work.tile([P, PACK], F32, name="d")
            nc.vector.scalar_tensor_tensor(
                out=d[:], in0=kept[("deg", g)][:], scalar=0.0, in1=kept[("inv", g)][:], op0=ALU.is_gt, op1=ALU.mult
            )
            kept[("d", g)] = d

        def spread(g):
            d = kept[("d", g)]
            d_free = ps_d.tile([P, NODES], F32, name="d_free")
            for j in range(PACK):
                nc.tensor.transpose(d_free[:, j * P : (j + 1) * P], d[:, j : j + 1].to_broadcast([P, P]), ident_f32[:])
            kept[("d_free", g)] = d_free

        def regroup_feat(g, half):
            f_grouped = double.tile([P, FEATS // 2, PACK], BF16, align_bytes=64, name="f_grouped")
            first = half * (FEATS // 2)
            f_columns = kept[("f_sb", g)][:, :, first : first + FEATS // 2].rearrange("p t c -> p c t")
            if 2 * g + half in RS:
                nc.scalar.copy(out=f_grouped[:], in_=f_columns)
            else:
                n = FEATS // 2 // F_PIECES
                for i in range(F_PIECES):
                    nc.gpsimd.tensor_scalar(
                        out=f_grouped[:, i * n : (i + 1) * n, :],
                        in0=f_columns[:, i * n : (i + 1) * n, :],
                        scalar1=1.0,
                        scalar2=0.0,
                        op0=ALU.mult,
                        op1=ALU.add,
                    )
            kept[("f_grouped", g, half)] = f_grouped

        def quantise_feat(g, half):
            kept[("f", g, half)] = quantise(deep, kept[("f_grouped", g, half)][:].rearrange("p c j -> p (c j)"), "f")

        def normalise(g, half):
            d = kept[("d", g)]
            d_free = kept[("d_free", g)]
            a_norm = work.tile([P, PAIR, NODES], BF16, name="a_norm")
            for a in range(PAIR):
                j = half * PAIR + a
                diagonal = slice(j * P, (j + 1) * P)
                pieces = [(diagonal, kept[("a_plus_i", g)][:, j, :])]
                for cols in (slice(0, j * P), slice((j + 1) * P, NODES)):
                    if cols.stop > cols.start:
                        pieces.append((cols, kept[("a_sb", g)][:, j, cols]))
                for cols, a_piece in pieces:
                    nc.vector.scalar_tensor_tensor(
                        out=a_norm[:, a, cols],
                        in0=a_piece,
                        scalar=d[:, j : j + 1],
                        in1=d_free[:, cols],
                        op0=ALU.mult,
                        op1=ALU.mult,
                    )
            kept[("a_norm", g, half)] = a_norm

        def transpose(g, half):
            a_norm = kept[("a_norm", g, half)]
            words = a_norm[:].rearrange("p a m -> p (a m)").bitcast(F32)
            a_t = ps_t.tile([P, PAIR, 2, P], F32, name="a_t")
            for a in range(PAIR):
                for u in range(2):
                    first = (2 * a + u) * P
                    nc.tensor.transpose(a_t[:, a, u, :], words[:, first : first + P], ident_f32[:])
            a_grouped = work.tile([P, PAIR, P, PACK], BF16, align_bytes=64, name="a_grouped")
            out_words = (
                a_grouped[:].rearrange("p a n t -> p (a n t)").bitcast(F32).rearrange("p (a n u) -> p a n u", a=PAIR, u=2)
            )
            in_words = a_t[:].rearrange("p a u n -> p a n u")
            if tiles_apart(g, half) == 1:
                nc.scalar.copy(out=out_words, in_=in_words)
            else:
                nc.scalar.copy(out=out_words[:, 0, :, :], in_=in_words[:, 0, :, :])
                nc.vector.tensor_copy(out=out_words[:, 1, :, :], in_=in_words[:, 1, :, :])
            kept[("a_grouped", g, half)] = a_grouped

        def quantise_a(g, half):
            kept[("a", g, half)] = quantise(work, kept[("a_grouped", g, half)][:].rearrange("p a n t -> p (a n t)"), "a", tiles_apart(g, half))
            kept[("h_grouped", g, half)] = work.tile([P, PAIR, P, PACK], BF16, align_bytes=64, name="h_grouped")

        def first_product(g, half, a):
            a_codes, a_scales = kept[("a", g, half)]
            h_t = ps_h.tile([P, PACK, P], F32, name="h_t")
            for t in range(PACK):
                f_codes, f_scales = kept[("f", g, t // PAIR)]
                f_cols = slice((t % PAIR) * P, (t % PAIR + 1) * P)
                nc.tensor.matmul_mx(
                    out=h_t[:, t, :],
                    lhsT=f_codes[:, f_cols].bitcast(FP8X4),
                    lhsT_scale=f_scales[:, f_cols],
                    rhs=a_codes[:, a * P : (a + 1) * P].bitcast(FP8X4),
                    rhs_scale=a_scales[:, a * P : (a + 1) * P],
                    start=True,
                    stop=True,
                )
            kept[("h_t", g, half, a)] = h_t

        def copy_h(g, half, a, engine_copy):
            engine_copy(
                out=kept[("h_grouped", g, half)][:, a, :, :],
                in_=kept[("h_t", g, half, a)][:].rearrange("p t n -> p n t"),
            )

        def quantise_h(g, half):
            kept[("h", g, half)] = quantise(work, kept[("h_grouped", g, half)][:].rearrange("p a n t -> p (a n t)"), "h", tiles_apart(g, half))
            kept[("result", g, half)] = work.tile([P, PAIR, OUTS], F32, name="result")

        def second_product(g, half, a):
            h_codes, h_scales = kept[("h", g, half)]
            o_ps = ps_o.tile([P, OUTS], F32, name="o_ps")
            nc.tensor.matmul_mx(
                out=o_ps[:],
                lhsT=h_codes[:, a * P : (a + 1) * P].bitcast(FP8X4),
                lhsT_scale=h_scales[:, a * P : (a + 1) * P],
                rhs=w_codes[:].bitcast(FP8X4),
                rhs_scale=w_scales[:],
                start=True,
                stop=True,
            )
            kept[("o_ps", g, half, a)] = o_ps

        def relu(g, half, a, on_vector):
            result = kept[("result", g, half)][:, a, :]
            o_ps = kept[("o_ps", g, half, a)]
            if on_vector:
                nc.vector.tensor_scalar_max(out=result, in0=o_ps[:], scalar1=0.0)
            else:
                nc.scalar.activation(out=result, in_=o_ps[:], func=ACT.Relu)

        def store(g, half):
            out_rows = out[g].rearrange("(j p) o -> p j o", j=PACK)
            apart = tiles_apart(g, half)
            for part in range(apart):
                first, n = part * PAIR // apart, PAIR // apart
                nc.sync.dma_start(
                    out=out_rows[:, half * PAIR + first : half * PAIR + first + n, :],
                    in_=kept[("result", g, half)][:, first : first + n, :],
                )

        def at(u, stage):
            if 0 <= u < HALVES:
                stage(u // 2, u % 2)

        def tick(s):
            k = s // 2
            even = s % 2 == 0
            def h_on_vector(s):
                return s >= H_TICK

            def o_on_vector(s):
                return s >= O_TICK


            def for_graph(g, stage):
                if 0 <= g < GRAPHS:
                    stage(g)

            at(s + 2 * AHEAD, load)

            if s == 0:
                sum_tiles(0, range(PACK))
            if even and s and s != 4:
                for_graph(k, sum_folded)
            if not even and s != 3:
                for_graph(k + 1, sum_tile)
            at(s - 3, normalise)
            if s == 3:
                for_graph(k + 1, sum_tile)
            if s == 4:
                for_graph(k, sum_folded)
            if s >= 6:
                at(s - 2, add_identity)
            if h_on_vector(s - 1):
                at(s - 5, lambda g, half: copy_h(g, half, 1, nc.vector.tensor_copy))
            if s == 1:
                at(0, add_identity)
            if not even:
                for_graph(k, inverse_roots)
            if s == 1:
                at(1, add_identity)
                mask_roots(0)
                at(2, add_identity)
                at(3, add_identity)
            if s == 4:
                for_graph(1, mask_roots)
            at(s - 4, quantise_a)
            if s == 5:
                quantise_w()
            if s == 4:
                at(0, quantise_feat)
            if s >= 4:
                at(s - 3, quantise_feat)
            at(s - 5, quantise_h)
            if not even and s > 3:
                for_graph(k, mask_roots)

            if o_on_vector(s - 1):
                at(s - 6, lambda g, half: relu(g, half, 1, True))
                at(s - 6, store)

            if s - 2 not in RS:
                at(s - 2, regroup_feat)

            if even:
                for_graph(k, roots)
            if not even and s != 3:
                for_graph(k + 1, fold)
            at(s - 3, transpose)
            if s - 2 in RS:
                at(s - 2, regroup_feat)
            if even:
                for_graph(k - 1, spread)
            if s == 3:
                for_graph(k + 1, fold)
            for a in range(PAIR):
                at(s - 4, lambda g, half: first_product(g, half, a))
                if not (h_on_vector(s) and a == 1):
                    at(s - 4, lambda g, half: copy_h(g, half, a, nc.scalar.copy))
            for a in range(PAIR):
                at(s - 5, lambda g, half: second_product(g, half, a))
                if not (o_on_vector(s) and a == 1):
                    at(s - 5, lambda g, half: relu(g, half, a, False))

            if not o_on_vector(s):
                at(s - 5, store)

        for s in range(HALVES + 6):
            tick(s)
            if s == 1:
                regroup_w()
